import numpy as np
import ml_dtypes


def mxq(x, axis, fmt="e4m3"):
    dtype, down = {"e4m3": (ml_dtypes.float8_e4m3fn, 7), "e5m2": (ml_dtypes.float8_e5m2, 14)}[fmt]
    v = np.moveaxis(np.asarray(x, np.float32).astype(ml_dtypes.bfloat16).astype(np.float64), axis, -1)
    blocks = v.reshape(v.shape[:-1] + (-1, 32))
    amax = np.abs(blocks).max(-1, keepdims=True)
    byte = np.maximum(np.where(amax > 0, np.frexp(amax)[1] - 1 + 127, 0) - down, 1)
    scale = np.exp2(byte - 127.0)
    codes = (blocks / scale).astype(np.float32).astype(dtype).astype(np.float64)
    return np.moveaxis((codes * scale).reshape(v.shape), -1, axis)


WIDE = False


def mx_kscale(k):
    if not WIDE:
        return np.ones(k)
    levels = np.array([18, -18])
    if k % 512:
        return np.exp2(np.random.permutation(np.resize(levels, k // 32))).repeat(32)
    a = np.empty((k // 512, 16))
    for p in range(k // 512):
        a[p, :8] = np.random.permutation(np.resize(levels, 8))
        for g in range(8):
            far = levels[np.abs(levels - a[p, g]) >= 10]
            a[p, g + 8] = far[np.random.randint(len(far))]
    return np.exp2(a.ravel()).repeat(32)


BF16 = ml_dtypes.bfloat16


def bf(x):
    return np.asarray(x, np.float32).astype(BF16)


def f64(x):
    return np.asarray(x).astype(np.float64)


N, IN_F, HID, OUT_F = 1536, 512, 512, 1024


def setup_inputs():
    u = mx_kscale(N)
    s = mx_kscale(N)
    v = mx_kscale(OUT_F)
    t = np.sqrt(u * s)
    g = 0.1 + 0.9 * np.random.random_sample(N)
    adj0 = bf(np.random.random_sample((N, N)) * g[:, None] * g[None, :])
    h1_0 = bf(np.random.standard_normal((N, HID)))
    W2_0 = bf(np.random.standard_normal((OUT_F, HID)) * 0.125 * np.sqrt(N / HID))
    b2 = bf(np.random.standard_normal(OUT_F) * 0.1)
    go = bf(np.random.standard_normal((N, OUT_F)) * np.exp2(np.random.randint(-6, 1, (N, 1))) * 8.0 * t[:, None] * v[None, :])
    r = np.power((f64(adj0) + np.eye(N)).sum(axis=1), -0.5)
    return {"h1": bf(f64(h1_0) / t[:, None]),
            "adj": bf(f64(adj0) / t[:, None] * t[None, :]),
            "W2": bf(f64(W2_0) / v[:, None]),
            "b2": b2,
            "r": np.asarray(r, np.float32),
            "grad_out": go}


def reference(h1, adj, W2, b2, r, grad_out):
    rf = f64(r)[:, None]
    dz2 = rf * f64(grad_out)
    back = (mxq(f64(adj), 0, "e4m3").T @ mxq(dz2, 0, "e5m2")) + dz2
    dz1 = rf * back
    dh1 = mxq(dz1, 1, "e5m2") @ mxq(f64(W2), 0, "e4m3")
    dW2 = mxq(dz1, 0, "e5m2").T @ mxq(f64(h1), 0, "e4m3")
    return dh1, dW2

@@ -1,0 +1,354 @@
+from contextlib import ExitStack
+
+import concourse.mybir as mybir
+from concourse.masks import make_identity
+
+NODES, HID, OUT_F = 1536, 512, 1024
+FLOPS = 2 * NODES * NODES * OUT_F + 4 * NODES * OUT_F * HID
+BYTES = 2 * (NODES * NODES + NODES * OUT_F + OUT_F * HID + NODES * HID) + 4 * NODES + 4 * (NODES * HID + OUT_F * HID)
+
+F32 = mybir.dt.float32
+BF16 = mybir.dt.bfloat16
+U32 = mybir.dt.uint32
+U8 = mybir.dt.uint8
+E4M3 = mybir.dt.float8_e4m3fn_x4
+E5M2 = mybir.dt.float8_e5m2_x4
+MULT = mybir.AluOpType.mult
+ADD = mybir.AluOpType.add
+COPY = mybir.ActivationFunctionType.Copy
+
+P = 128
+G = NODES // 512
+CH = OUT_F // 512
+
+
+def tile_gcnlayer_pa_v_kernel(tc, h1, adj, W2, b2, r, grad_out, out_0, out_1):
+    nc = tc.nc
+    adj_v = adj.rearrange("(g p i) j -> g p i j", p=P, i=4)
+    go_v = grad_out.rearrange("(g p i) c -> g p i c", p=P, i=4)
+    h1_v = h1.rearrange("(g p i) h -> g p i h", p=P, i=4)
+    w2_v = W2.rearrange("(g p i) h -> g p i h", p=P, i=4)
+    out0_v = out_0.rearrange("(g p t) h -> g p t h", p=P, t=4)
+
+    with ExitStack() as ctx:
+        keep = ctx.enter_context(tc.tile_pool(name="keep", bufs=1))
+        rawp = ctx.enter_context(tc.tile_pool(name="raw", bufs=9))
+        work = ctx.enter_context(tc.tile_pool(name="work", bufs=3))
+        psum = ctx.enter_context(tc.psum_pool(name="psum", bufs=1))
+
+        r_sb = keep.tile([P, G, 4], F32, name="r_sb")
+        r2_sb = keep.tile([P, G, 4], F32, name="r2_sb")
+        ident = keep.tile([P, P], F32, name="ident")
+        ident_b = keep.tile([P, P], BF16, name="ident_b")
+        go_sb = {}
+        raw = {}
+        codes = {}
+        grouped = {}
+        dz2b = {}
+        dz1 = {}
+        q = {}
+        acc = {}
+
+        nc.scalar.dma_start(out=r_sb[:], in_=r.rearrange("(g p t) -> p g t", p=P, t=4))
+
+        def load_go(g, c):
+            cs = slice(512 * c, 512 * c + 512)
+            go_sb[g, c] = keep.tile([P, 4, 512], BF16, name="go_%d_%d" % (g, c), align_bytes=64)
+            nc.sync.dma_start(out=go_sb[g, c][:], in_=go_v[g][:, :, cs])
+
+        def load(key, view):
+            t = rawp.tile([P, 4, 512], BF16, name="raw_chunk", align_bytes=64)
+            nc.sync.dma_start(out=t[:], in_=view)
+            raw[key] = t
+
+        def load_adj(g, j):
+            load(("a", g, j), adj_v[g][:, :, 512 * j : 512 * j + 512])
+
+        for g in range(G):
+            load_go(g, 0)
+            load_adj(g, 0)
+        for g in range(G):
+            load_adj(g, 1)
+        for g in range(G):
+            load_adj(g, 2)
+        for g in range(G):
+            load_go(g, 1)
+
+        make_identity(nc, ident_b[:])
+        make_identity(nc, ident[:])
+        nc.vector.tensor_tensor(out=r2_sb[:], in0=r_sb[:], in1=r_sb[:], op=MULT)
+
+        def copy_on(eng, out, in_):
+            if eng == "v":
+                nc.vector.tensor_copy(out=out, in_=in_)
+            else:
+                nc.scalar.copy(out=out, in_=in_)
+
+        def scale(g, c):
+            t = work.tile([P, 4, 512], BF16, name="dz2b", align_bytes=64)
+            for i in range(4):
+                nc.vector.tensor_scalar(out=t[:, i, :], in0=go_sb[g, c][:, i, :],
+                                        scalar1=r_sb[:, g, i : i + 1], scalar2=None, op0=MULT)
+            dz2b[g, c] = t
+
+        def interleave(eng, key, src):
+            t = work.tile([P, 512, 4], BF16, name="grouped", bufs=5, align_bytes=64)
+            copy_on(eng, t[:].rearrange("p (c i) t -> p c t i", i=4), src.rearrange("p t (c i) -> p c t i", i=4))
+            grouped[key] = t
+
+        def interleave_n(engs, j, c):
+            t = work.tile([P, 512, 4], BF16, name="grouped", bufs=5, align_bytes=64)
+            for u in range(2):
+                copy_on(engs[u], t[:].rearrange("p (m u e) t -> p m u t e", u=2, e=2)[:, :, u],
+                        dz1[j, c][:].rearrange("p t (u m e) -> p u m t e", u=2, e=2)[:, u])
+            grouped["n", j, c] = t
+
+        def interleave_adj(eng, key):
+            t = work.tile([P, 512, 4], BF16, name="grouped", bufs=5, align_bytes=64)
+            copy_on(eng, t[:].rearrange("p (t m) i -> p m i t", t=4), raw[key][:].rearrange("p i (m t) -> p m i t", t=4))
+            grouped[key] = t
+
+        moved = {}
+
+        def move(key):
+            banks = []
+            for half in range(2):
+                x = psum.tile([P, 2, 512], BF16, name="misc", bufs=4)
+                for k in range(2):
+                    if key[0] == "a":
+                        src = raw[key][:].rearrange("p i (m t) -> p t m i", t=4)[:, 2 * half + k]
+                        dst = x[:, k, :].rearrange("p (m i) -> p m i", i=4)
+                    else:
+                        src = dz2b[key[1:]][:].rearrange("p i (m u e) -> p u m e i", u=2, e=2)[:, half, 64 * k : 64 * k + 64]
+                        dst = x[:, k, :].rearrange("p (m e i) -> p m e i", e=2, i=4)
+                    nc.tensor.matmul(dst, lhsT=ident_b[:], rhs=src, start=True, stop=True)
+                banks.append(x)
+            moved[key] = banks
+
+        def moved_out(engs, key):
+            t = work.tile([P, 512, 4], BF16, name="grouped", bufs=5, align_bytes=64)
+            dst = t[:].rearrange("p w t -> p (w t)").rearrange("p (h k n) -> p h k n", h=2, k=2)
+            for half in range(2):
+                copy_on(engs[half], dst[:, half], moved[key][half][:])
+            grouped[key] = t
+
+        def quant(key, fmt):
+            tag = "_".join([str(k) for k in key])
+            c = keep.tile([P, 512], U32, name="codes_" + tag, align_bytes=64)
+            s = keep.tile([P, 512], U8, name="scales_" + tag, align_bytes=64)
+            nc.vector.quantize_mx(out=c[:].bitcast(fmt), scales=s[:], in_=grouped[key][:].rearrange("p w t -> p (w t)"))
+            codes[key] = (c, s, fmt)
+
+        def prep(eng, key):
+            if key[0] == "a":
+                interleave_adj(eng, key)
+            elif key[0] == "z":
+                interleave(eng, key, dz2b[key[1:]][:])
+            else:
+                interleave(eng, key, raw[key][:])
+
+        def mx(out, left, m0, right, start, stop):
+            lc, ls, lf = codes[left]
+            rc, rs, rf = codes[right]
+            nc.tensor.matmul_mx(out=out, lhsT=lc[:, m0 : m0 + P].bitcast(lf), lhsT_scale=ls[:, m0 : m0 + P],
+                                rhs=rc[:].bitcast(rf), rhs_scale=rs[:], start=start, stop=stop)
+
+        def new_misc():
+            return psum.tile([P, 512], F32, name="misc", bufs=4)
+
+        def new_acc():
+            return psum.tile([P, 512], F32, name="acc", bufs=4)
+
+        def r_open(j, c):
+            for t in range(4):
+                acc[j, c, t] = new_acc()
+
+        def r_pass(j, c, t, g):
+            mx(acc[j, c, t][:], ("a", g, j), P * t, ("z", g, c), g == 0, g == G - 1)
+
+        def r_group(j, c, t):
+            acc[j, c, t] = new_acc()
+            for g in range(G):
+                r_pass(j, c, t, g)
+
+        def make_q(j, c, t, eng="v"):
+            x = work.tile([P, 512], F32, name="q", bufs=6)
+            dst = x[:].rearrange("p (u m e) -> p u m e", u=2, e=2)
+            src = go_sb[j, c][:, t, :].rearrange("p (m u e) -> p u m e", u=2, e=2)
+            if eng == "v":
+                nc.vector.tensor_scalar(out=dst, in0=src, scalar1=r2_sb[:, j, t : t + 1], scalar2=None, op0=MULT)
+            else:
+                nc.scalar.activation(out=dst, in_=src, func=COPY, scale=r2_sb[:, j, t : t + 1])
+            q[j, c, t] = x
+
+        def stt(j, c, t):
+            if (j, c) not in dz1:
+                dz1[j, c] = work.tile([P, 4, 512], BF16, name="dz1", bufs=3, align_bytes=64)
+            nc.vector.scalar_tensor_tensor(out=dz1[j, c][:, t, :], in0=acc[j, c, t][:], scalar=r_sb[:, j, t : t + 1],
+                                           in1=q[j, c, t][:], op0=MULT, op1=ADD)
+
+        xt = {}
+
+        def turn(j, c, half):
+            x = new_misc()[:].rearrange("p (k u m) -> p k u m", k=2, u=2)
+            for k in range(2):
+                words = dz1[j, c][:, 2 * half + k, :].bitcast(F32)
+                for u in range(2):
+                    nc.tensor.transpose(x[:, k, u, :], words[:, P * u : P * u + P], ident[:])
+            xt[j, c, half] = x
+
+        def turn_out(eng, j, c, half):
+            key = ("c", j, c)
+            if key not in grouped:
+                grouped[key] = work.tile([P, 512, 4], BF16, name="grouped_c", bufs=2, align_bytes=64)
+            dst = grouped[key][:].rearrange("p w t -> p (w t)").bitcast(F32)
+            copy_on(eng, dst.rearrange("p (h k m u) -> p h k m u", h=2, k=2, u=2)[:, half],
+                    xt[j, c, half].rearrange("p k u m -> p k m u"))
+
+        o0 = {}
+
+        def out0_group(j, t):
+            a = new_misc()
+            for c in range(CH):
+                mx(a[:], ("c", j, c), P * t, ("w", c), c == 0, c == CH - 1)
+            acc["o0", j, t] = a
+
+        def out0_evac(eng, j, t):
+            if j not in o0:
+                o0[j] = work.tile([P, 4, 512], F32, name="o0", bufs=2)
+            copy_on(eng, o0[j][:, t, :], acc["o0", j, t][:])
+            if t % 2 == 1:
+                nc.sync.dma_start(out=out0_v[j][:, t - 1 : t + 1, :], in_=o0[j][:, t - 1 : t + 1, :])
+
+        def out1_pass(cb, g, new):
+            if g == 0:
+                acc["o1", cb] = new()
+            mx(acc["o1", cb][:], ("n", g, cb // 4), P * (cb % 4), ("h", g), g == 0, g == G - 1)
+
+        def out1_evac(eng, cb):
+            x = work.tile([P, 512], F32, name="o1", bufs=4)
+            copy_on(eng, x[:], acc["o1", cb][:])
+            nc.sync.dma_start(out=out_1[P * cb : P * cb + P, :], in_=x[:])
+
+        def through_psum(key, engs="ss"):
+            move(key)
+            moved_out(engs, key)
+
+        rounds = [(j, c) for c in range(CH) for j in range(G)]
+
+        def r_passes(k, g):
+            for t in range(4):
+                r_pass(*rounds[k], t, g)
+
+        r_open(0, 0)
+        scale(0, 0)
+        through_psum(("z", 0, 0))
+        through_psum(("a", 0, 0))
+        scale(1, 0)
+        through_psum(("z", 1, 0))
+        quant(("z", 0, 0), E5M2)
+        quant(("a", 0, 0), E4M3)
+        make_q(0, 0, 0, "s")
+        make_q(0, 0, 1, "s")
+        through_psum(("a", 1, 0))
+        r_passes(0, 0)
+        scale(2, 0)
+        through_psum(("z", 2, 0))
+        quant(("z", 1, 0), E5M2)
+        quant(("a", 1, 0), E4M3)
+        make_q(0, 0, 2, "s")
+        make_q(0, 0, 3, "s")
+        through_psum(("a", 2, 0))
+        r_passes(0, 1)
+        quant(("z", 2, 0), E5M2)
+        prep("v", ("a", 0, 1))
+        quant(("a", 2, 0), E4M3)
+        through_psum(("a", 1, 1))
+        r_passes(0, 2)
+        prep("v", ("a", 2, 1))
+        quant(("a", 0, 1), E4M3)
+        through_psum(("a", 0, 2))
+        prep("s", ("a", 2, 2))
+        stt(0, 0, 0)
+        stt(0, 0, 1)
+        quant(("a", 1, 1), E4M3)
+        stt(0, 0, 2)
+        stt(0, 0, 3)
+        quant(("a", 2, 1), E4M3)
+        for t in range(4):
+            r_group(*rounds[1], t)
+
+        extra = [
+            [("a", 1, 2, "p")],
+            [("z", 0, 1, "p"), ("z", 1, 1, "p"), ("z", 2, 1, "p")],
+            [("h", 0, "v"), ("h", 1, "s")],
+            [("h", 2, "s"), ("w", 0, "v")],
+            [("w", 1, "s")],
+            [],
+        ]
+        n_eng = ["vv", "vv", "vv", "vv", "vv", "vv"]
+        q_eng = "ssssss"
+        for k in range(6):
+            j, c = rounds[k]
+            if k == 1:
+                for g in range(G):
+                    load(("h", g), h1_v[g])
+                for g in range(CH):
+                    load(("w", g), w2_v[g])
+            for e in extra[k]:
+                if e[0] == "z":
+                    scale(*e[1:3])
+                if e[-1] == "p":
+                    through_psum(e[:-1])
+                elif e[-1] == "s":
+                    prep(e[-1], e[:-1])
+            if k > 0:
+                for t in range(4):
+                    stt(j, c, t)
+            else:
+                quant(("a", 0, 2), E4M3)
+                quant(("a", 2, 2), E4M3)
+            if k < 5:
+                for t in range(4):
+                    make_q(*rounds[k + 1], t, q_eng[k])
+                if k > 0:
+                    for t in range(4):
+                        r_group(*rounds[k + 1], t)
+            if k == 5:
+                for g in range(2):
+                    for cb in range(4, 8):
+                        out1_pass(cb, g, new_acc)
+            for half in range(2):
+                turn(j, c, half)
+            for e in extra[k]:
+                if e[-1] == "v":
+                    prep(e[-1], e[:-1])
+            if 0 < k < 5:
+                quant(("c", *rounds[k - 1]), E5M2)
+            interleave_n(n_eng[k], j, c)
+            for e in extra[k]:
+                quant(e[:-1], E5M2 if e[0] == "z" else E4M3)
+            for half in range(2):
+                turn_out("s", j, c, half)
+            if k == 4:
+                for t in range(4):
+                    out0_group(0, t)
+                    out0_evac("s", 0, t)
+                quant(("c", *rounds[4]), E5M2)
+                for t in range(4):
+                    out0_group(1, t)
+                    out0_evac("s", 1, t)
+            if k == 5:
+                quant(("c", *rounds[5]), E5M2)
+            quant(("n", j, c), E5M2)
+            if k == 3:
+                for cb in range(4):
+                    for g in range(G):
+                        out1_pass(cb, g, new_misc)
+                    out1_evac("s", cb)
+        for t in range(4):
+            out0_group(2, t)
+            out0_evac("sv"[t % 2], 2, t)
+        for cb in range(4, 8):
+            out1_pass(cb, 2, new_acc)
+            out1_evac("sv"[cb % 2], cb)

@@ -35,11 +35,11 @@ def tile_gcnlayer_pa_v_kernel(tc, h1, adj, W2, b2, r, grad_out, out_0, out_1):
         rawp = ctx.enter_context(tc.tile_pool(name="raw", bufs=9))
         work = ctx.enter_context(tc.tile_pool(name="work", bufs=3))
         psum = ctx.enter_context(tc.psum_pool(name="psum", bufs=1))
+        ctx.enter_context(tc.manual_schedule(engines={mybir.EngineType.PE}))
 
         r_sb = keep.tile([P, G, 4], F32, name="r_sb")
         r2_sb = keep.tile([P, G, 4], F32, name="r2_sb")
         ident = keep.tile([P, P], F32, name="ident")
-        ident_b = keep.tile([P, P], BF16, name="ident_b")
         go_sb = {}
         raw = {}
         codes = {}
@@ -74,7 +74,6 @@ def tile_gcnlayer_pa_v_kernel(tc, h1, adj, W2, b2, r, grad_out, out_0, out_1):
         for g in range(G):
             load_go(g, 1)
 
-        make_identity(nc, ident_b[:])
         make_identity(nc, ident[:])
         nc.vector.tensor_tensor(out=r2_sb[:], in0=r_sb[:], in1=r_sb[:], op=MULT)
 
@@ -96,40 +95,9 @@ def tile_gcnlayer_pa_v_kernel(tc, h1, adj, W2, b2, r, grad_out, out_0, out_1):
             copy_on(eng, t[:].rearrange("p (c i) t -> p c t i", i=4), src.rearrange("p t (c i) -> p c t i", i=4))
             grouped[key] = t
 
-        def interleave_n(engs, j, c):
-            t = work.tile([P, 512, 4], BF16, name="grouped", bufs=5, align_bytes=64)
-            for u in range(2):
-                copy_on(engs[u], t[:].rearrange("p (m u e) t -> p m u t e", u=2, e=2)[:, :, u],
-                        dz1[j, c][:].rearrange("p t (u m e) -> p u m t e", u=2, e=2)[:, u])
-            grouped["n", j, c] = t
-
         def interleave_adj(eng, key):
             t = work.tile([P, 512, 4], BF16, name="grouped", bufs=5, align_bytes=64)
             copy_on(eng, t[:].rearrange("p (t m) i -> p m i t", t=4), raw[key][:].rearrange("p i (m t) -> p m i t", t=4))
-            grouped[key] = t
-
-        moved = {}
-
-        def move(key):
-            banks = []
-            for half in range(2):
-                x = psum.tile([P, 2, 512], BF16, name="misc", bufs=4)
-                for k in range(2):
-                    if key[0] == "a":
-                        src = raw[key][:].rearrange("p i (m t) -> p t m i", t=4)[:, 2 * half + k]
-                        dst = x[:, k, :].rearrange("p (m i) -> p m i", i=4)
-                    else:
-                        src = dz2b[key[1:]][:].rearrange("p i (m u e) -> p u m e i", u=2, e=2)[:, half, 64 * k : 64 * k + 64]
-                        dst = x[:, k, :].rearrange("p (m e i) -> p m e i", e=2, i=4)
-                    nc.tensor.matmul(dst, lhsT=ident_b[:], rhs=src, start=True, stop=True)
-                banks.append(x)
-            moved[key] = banks
-
-        def moved_out(engs, key):
-            t = work.tile([P, 512, 4], BF16, name="grouped", bufs=5, align_bytes=64)
-            dst = t[:].rearrange("p w t -> p (w t)").rearrange("p (h k n) -> p h k n", h=2, k=2)
-            for half in range(2):
-                copy_on(engs[half], dst[:, half], moved[key][half][:])
             grouped[key] = t
 
         def quant(key, fmt):
@@ -173,8 +141,8 @@ def tile_gcnlayer_pa_v_kernel(tc, h1, adj, W2, b2, r, grad_out, out_0, out_1):
 
         def make_q(j, c, t, eng="v"):
             x = work.tile([P, 512], F32, name="q", bufs=6)
-            dst = x[:].rearrange("p (u m e) -> p u m e", u=2, e=2)
-            src = go_sb[j, c][:, t, :].rearrange("p (m u e) -> p u m e", u=2, e=2)
+            dst = x[:]
+            src = go_sb[j, c][:, t, :]
             if eng == "v":
                 nc.vector.tensor_scalar(out=dst, in0=src, scalar1=r2_sb[:, j, t : t + 1], scalar2=None, op0=MULT)
             else:
@@ -194,7 +162,7 @@ def tile_gcnlayer_pa_v_kernel(tc, h1, adj, W2, b2, r, grad_out, out_0, out_1):
             for k in range(2):
                 words = dz1[j, c][:, 2 * half + k, :].bitcast(F32)
                 for u in range(2):
-                    nc.tensor.transpose(x[:, k, u, :], words[:, P * u : P * u + P], ident[:])
+                    nc.tensor.transpose(x[:, k, u, :], words[:, u::2], ident[:])
             xt[j, c, half] = x
 
         def turn_out(eng, j, c, half):
@@ -230,10 +198,6 @@ def tile_gcnlayer_pa_v_kernel(tc, h1, adj, W2, b2, r, grad_out, out_0, out_1):
             copy_on(eng, x[:], acc["o1", cb][:])
             nc.sync.dma_start(out=out_1[P * cb : P * cb + P, :], in_=x[:])
 
-        def through_psum(key, engs="ss"):
-            move(key)
-            moved_out(engs, key)
-
         rounds = [(j, c) for c in range(CH) for j in range(G)]
 
         def r_passes(k, g):
@@ -241,53 +205,31 @@ def tile_gcnlayer_pa_v_kernel(tc, h1, adj, W2, b2, r, grad_out, out_0, out_1):
                 r_pass(*rounds[k], t, g)
 
         r_open(0, 0)
-        scale(0, 0)
-        through_psum(("z", 0, 0))
-        through_psum(("a", 0, 0))
-        scale(1, 0)
-        through_psum(("z", 1, 0))
-        quant(("z", 0, 0), E5M2)
-        quant(("a", 0, 0), E4M3)
-        make_q(0, 0, 0, "s")
-        make_q(0, 0, 1, "s")
-        through_psum(("a", 1, 0))
-        r_passes(0, 0)
-        scale(2, 0)
-        through_psum(("z", 2, 0))
-        quant(("z", 1, 0), E5M2)
-        quant(("a", 1, 0), E4M3)
-        make_q(0, 0, 2, "s")
-        make_q(0, 0, 3, "s")
-        through_psum(("a", 2, 0))
-        r_passes(0, 1)
-        quant(("z", 2, 0), E5M2)
-        prep("v", ("a", 0, 1))
-        quant(("a", 2, 0), E4M3)
-        through_psum(("a", 1, 1))
-        r_passes(0, 2)
-        prep("v", ("a", 2, 1))
-        quant(("a", 0, 1), E4M3)
-        through_psum(("a", 0, 2))
-        prep("s", ("a", 2, 2))
-        stt(0, 0, 0)
-        stt(0, 0, 1)
-        quant(("a", 1, 1), E4M3)
-        stt(0, 0, 2)
-        stt(0, 0, 3)
-        quant(("a", 2, 1), E4M3)
+        for g in range(G):
+            scale(g, 0)
+            if g:
+                quant(("z", g - 1, 0), E5M2)
+            prep("v", ("z", g, 0))
+            prep("s", ("a", g, 0))
+            if g:
+                quant(("a", g - 1, 0), E4M3)
+                r_passes(0, g - 1)
         for t in range(4):
-            r_group(*rounds[1], t)
+            make_q(0, 0, t, "s")
+        prep("v", ("a", 0, 1))
+        quant(("z", 2, 0), E5M2)
+        quant(("a", 2, 0), E4M3)
+        r_passes(0, 2)
+        quant(("a", 0, 1), E4M3)
 
         extra = [
-            [("a", 1, 2, "p")],
-            [("z", 0, 1, "p"), ("z", 1, 1, "p"), ("z", 2, 1, "p")],
-            [("h", 0, "v"), ("h", 1, "s")],
-            [("h", 2, "s"), ("w", 0, "v")],
-            [("w", 1, "s")],
+            [("a", 1, 1, "s"), ("a", 2, 1, "s")],
+            [("a", 0, 2, "s"), ("a", 1, 2, "s"), ("a", 2, 2, "v")],
+            [("z", 0, 1, "s"), ("z", 1, 1, "v"), ("z", 2, 1, "s")],
+            [("h", 0, "v"), ("h", 1, "s"), ("h", 2, "s")],
+            [("w", 0, "v"), ("w", 1, "s")],
             [],
         ]
-        n_eng = ["vv", "vv", "vv", "vv", "vv", "vv"]
-        q_eng = "ssssss"
         for k in range(6):
             j, c = rounds[k]
             if k == 1:
@@ -298,54 +240,49 @@ def tile_gcnlayer_pa_v_kernel(tc, h1, adj, W2, b2, r, grad_out, out_0, out_1):
             for e in extra[k]:
                 if e[0] == "z":
                     scale(*e[1:3])
-                if e[-1] == "p":
-                    through_psum(e[:-1])
-                elif e[-1] == "s":
+                if e[-1] == "s":
+                    prep(e[-1], e[:-1])
+            for t in range(4):
+                stt(j, c, t)
+            for e in extra[k]:
+                if e[-1] == "v":
                     prep(e[-1], e[:-1])
             if k > 0:
-                for t in range(4):
-                    stt(j, c, t)
-            else:
-                quant(("a", 0, 2), E4M3)
-                quant(("a", 2, 2), E4M3)
+                quant(("c", *rounds[k - 1]), E5M2)
             if k < 5:
                 for t in range(4):
-                    make_q(*rounds[k + 1], t, q_eng[k])
-                if k > 0:
-                    for t in range(4):
-                        r_group(*rounds[k + 1], t)
-            if k == 5:
+                    make_q(*rounds[k + 1], t, "s")
+            if k == 0:
+                interleave("v", ("n", j, c), dz1[j, c][:])
+            for e in extra[k]:
+                quant(e[:-1], E5M2 if e[0] == "z" else E4M3)
+            if k > 0:
+                interleave("v", ("n", j, c), dz1[j, c][:])
+            if k < 5:
+                for t in range(4):
+                    r_group(*rounds[k + 1], t)
+            else:
                 for g in range(2):
                     for cb in range(4, 8):
                         out1_pass(cb, g, new_acc)
             for half in range(2):
                 turn(j, c, half)
-            for e in extra[k]:
-                if e[-1] == "v":
-                    prep(e[-1], e[:-1])
-            if 0 < k < 5:
-                quant(("c", *rounds[k - 1]), E5M2)
-            interleave_n(n_eng[k], j, c)
-            for e in extra[k]:
-                quant(e[:-1], E5M2 if e[0] == "z" else E4M3)
             for half in range(2):
                 turn_out("s", j, c, half)
             if k == 4:
-                for t in range(4):
-                    out0_group(0, t)
-                    out0_evac("s", 0, t)
-                quant(("c", *rounds[4]), E5M2)
-                for t in range(4):
-                    out0_group(1, t)
-                    out0_evac("s", 1, t)
-            if k == 5:
-                quant(("c", *rounds[5]), E5M2)
-            quant(("n", j, c), E5M2)
-            if k == 3:
                 for cb in range(4):
                     for g in range(G):
                         out1_pass(cb, g, new_misc)
                     out1_evac("s", cb)
+                for t in range(4):
+                    out0_group(0, t)
+                    out0_evac("s", 0, t)
+            if k == 5:
+                for t in range(4):
+                    out0_group(1, t)
+                    out0_evac("s", 1, t)
+                quant(("c", *rounds[5]), E5M2)
+            quant(("n", j, c), E5M2)
         for t in range(4):
             out0_group(2, t)
             out0_evac("sv"[t % 2], 2, t)

@@ -4,8 +4,8 @@ import concourse.mybir as mybir
 from concourse.masks import make_identity
 
 NODES, HID, OUT_F = 1536, 512, 1024
-FLOPS = 2 * NODES * NODES * OUT_F + 4 * NODES * OUT_F * HID
-BYTES = 2 * (NODES * NODES + NODES * OUT_F + OUT_F * HID + NODES * HID) + 4 * NODES + 4 * (NODES * HID + OUT_F * HID)
+FLOPS = 2 * NODES * NODES * OUT_F + 2 * (2 * NODES * OUT_F * HID)
+BYTES = 2 * (NODES * NODES + NODES * OUT_F + OUT_F * HID + NODES * HID) + 4 * (NODES + NODES * HID + OUT_F * HID)
 
 F32 = mybir.dt.float32
 BF16 = mybir.dt.bfloat16
@@ -18,274 +18,368 @@ ADD = mybir.AluOpType.add
 COPY = mybir.ActivationFunctionType.Copy
 
 P = 128
-G = NODES // 512
-CH = OUT_F // 512
+ROWS = 4
+W = P * ROWS
+TILES = W // P
+G = NODES // W
+C = OUT_F // W
+BANKS = 4
+
+V, S, GP, VS = "v", "s", "g", "vs"
+ALL = (0, 1, 2, 3)
+LAST_STORED = 1
 
 
 def tile_gcnlayer_pa_v_kernel(tc, h1, adj, W2, b2, r, grad_out, out_0, out_1):
     nc = tc.nc
-    adj_v = adj.rearrange("(g p i) j -> g p i j", p=P, i=4)
-    go_v = grad_out.rearrange("(g p i) c -> g p i c", p=P, i=4)
-    h1_v = h1.rearrange("(g p i) h -> g p i h", p=P, i=4)
-    w2_v = W2.rearrange("(g p i) h -> g p i h", p=P, i=4)
-    out0_v = out_0.rearrange("(g p t) h -> g p t h", p=P, t=4)
+    copy_on = {V: nc.vector.tensor_copy, S: nc.scalar.copy}
+
+    adj_v = adj.rearrange("(g p i) j -> g p i j", p=P, i=ROWS)
+    go_v = grad_out.rearrange("(g p i) c -> g p i c", p=P, i=ROWS)
+    h1_v = h1.rearrange("(g p i) h -> g p i h", p=P, i=ROWS)
+    w2_v = W2.rearrange("(g p i) h -> g p i h", p=P, i=ROWS)
+    out0_v = out_0.rearrange("(g p i) h -> g p i h", p=P, i=ROWS)
 
     with ExitStack() as ctx:
         keep = ctx.enter_context(tc.tile_pool(name="keep", bufs=1))
         rawp = ctx.enter_context(tc.tile_pool(name="raw", bufs=9))
-        work = ctx.enter_context(tc.tile_pool(name="work", bufs=3))
-        psum = ctx.enter_context(tc.psum_pool(name="psum", bufs=1))
-        ctx.enter_context(tc.manual_schedule(engines={mybir.EngineType.PE}))
+        work = ctx.enter_context(tc.tile_pool(name="work", bufs=2))
+        psum = ctx.enter_context(tc.psum_pool(name="psum", bufs=BANKS))
+        ctx.enter_context(tc.manual_schedule())
 
-        r_sb = keep.tile([P, G, 4], F32, name="r_sb")
-        r2_sb = keep.tile([P, G, 4], F32, name="r2_sb")
+        r_sb = keep.tile([P, G, ROWS], F32, name="r_sb")
+        r2_sb = keep.tile([P, G, ROWS], F32, name="r2_sb")
         ident = keep.tile([P, P], F32, name="ident")
-        go_sb = {}
+        ident_b = keep.tile([P, P], BF16, name="ident_b")
+
         raw = {}
-        codes = {}
         grouped = {}
-        dz2b = {}
+        codes = {}
+        moving = {}
         dz1 = {}
-        q = {}
-        acc = {}
-
-        nc.scalar.dma_start(out=r_sb[:], in_=r.rearrange("(g p t) -> p g t", p=P, t=4))
-
-        def load_go(g, c):
-            cs = slice(512 * c, 512 * c + 512)
-            go_sb[g, c] = keep.tile([P, 4, 512], BF16, name="go_%d_%d" % (g, c), align_bytes=64)
-            nc.sync.dma_start(out=go_sb[g, c][:], in_=go_v[g][:, :, cs])
+        self_loop = {}
+        marks = {}
+        sums = {}
+        flipped = {}
+        rows0 = {}
 
         def load(key, view):
-            t = rawp.tile([P, 4, 512], BF16, name="raw_chunk", align_bytes=64)
-            nc.sync.dma_start(out=t[:], in_=view)
-            raw[key] = t
+            raw[key] = rawp.tile([P, ROWS, W], BF16, name="raw_chunk", align_bytes=64)
+            nc.sync.dma_start(out=raw[key][:], in_=view)
 
         def load_adj(g, j):
-            load(("a", g, j), adj_v[g][:, :, 512 * j : 512 * j + 512])
+            load(("adj", g, j), adj_v[g][:, :, W * j : W * j + W])
 
+        def load_grad_out(g, c):
+            raw["go", g, c] = keep.tile([P, ROWS, W], BF16, name="go_%d_%d" % (g, c), align_bytes=64)
+            nc.sync.dma_start(out=raw["go", g, c][:], in_=go_v[g][:, :, W * c : W * c + W])
+
+        def scale_by_r(g, c):
+            raw["dz2", g, c] = work.tile([P, ROWS, W], BF16, name="dz2", bufs=3, align_bytes=64)
+            for i in range(ROWS):
+                nc.vector.tensor_scalar(out=raw["dz2", g, c][:, i, :], in0=raw["go", g, c][:, i, :],
+                                        scalar1=r_sb[:, g, i : i + 1], scalar2=None, op0=MULT)
+
+        def new_grouped():
+            return work.tile([P, W, ROWS], BF16, name="grouped", bufs=6, align_bytes=64)
+
+        def interleave(engines, key):
+            grouped[key] = new_grouped()
+            if key[0] == "adj":
+                dst = grouped[key][:].rearrange("p (t a m) i -> p a t m i", t=TILES, m=2)
+                src = raw[key][:].rearrange("p i (a m t) -> p a t m i", m=2, t=TILES)
+                share = TILES // len(engines)
+                for n, e in enumerate(engines):
+                    part = slice(share * n, share * n + share)
+                    copy_on[e](out=dst[:, :, part], in_=src[:, :, part])
+            else:
+                dst = grouped[key][:].rearrange("p (w n) i -> p w i n", n=4)
+                src = (dz1[key[1:]] if key[0] == "nodes" else raw[key])[:].rearrange("p i (w n) -> p w i n", n=4)
+                share = W // 4 // len(engines)
+                for n, e in enumerate(engines):
+                    part = slice(share * n, share * n + share)
+                    copy_on[e](out=dst[:, part], in_=src[:, part])
+
+        def move(key):
+            for half in range(2):
+                bank = psum.tile([P, ROWS * W // 2], BF16, name="mixed")
+                cols = slice(W // 2 * half, W // 2 * half + W // 2)
+                if key[0] == "adj":
+                    dst = bank[:].rearrange("p (t m i) -> p i m t", t=TILES, i=ROWS)
+                else:
+                    dst = bank[:].rearrange("p (w i) -> p i w", i=ROWS)
+                for i in range(0, ROWS, 2):
+                    src = raw[key][:, i : i + 2, cols]
+                    if key[0] == "adj":
+                        src = src.rearrange("p i (m t) -> p i m t", t=TILES)
+                    nc.tensor.matmul(dst[:, i : i + 2], lhsT=ident_b[:], rhs=src, start=True, stop=True)
+                moving[key, half] = bank
+
+        def moved(key, halves):
+            for half in halves:
+                if half == 0:
+                    grouped[key] = new_grouped()
+                cols = slice(W // 2 * half, W // 2 * half + W // 2)
+                bank = moving[key, half]
+                if key[0] == "adj":
+                    dst = grouped[key][:].rearrange("p (t m) i -> p t (m i)", t=TILES)[:, :, cols]
+                    nc.scalar.copy(out=dst, in_=bank[:].rearrange("p (t n) -> p t n", t=TILES))
+                else:
+                    nc.scalar.copy(out=grouped[key][:, cols, :].rearrange("p w i -> p (w i)"), in_=bank[:])
+
+        def quantise(key):
+            fmt = E5M2 if key[0] in ("dz2", "nodes", "feats") else E4M3
+            tag = "_".join([str(k) for k in key])
+            words = keep.tile([P, W], U32, name="words_" + tag, align_bytes=64)
+            scales = keep.tile([P, W], U8, name="scales_" + tag, align_bytes=64)
+            nc.vector.quantize_mx(out=words[:].bitcast(fmt), scales=scales[:],
+                                  in_=grouped[key][:].rearrange("p w i -> p (w i)"))
+            codes[key] = (words, scales, fmt)
+
+        def mx_pass(out, left, block, right, start, stop):
+            lw, ls, lf = codes[left]
+            rw, rs, rf = codes[right]
+            cols = slice(P * block, P * block + P)
+            nc.tensor.matmul_mx(out=out, lhsT=lw[:, cols].bitcast(lf), lhsT_scale=ls[:, cols],
+                                rhs=rw[:].bitcast(rf), rhs_scale=rs[:], start=start, stop=stop)
+
+        def new_bank(tag):
+            return psum.tile([P, W], F32, name=tag)
+
+        def first_pass(g):
+            for t in ALL:
+                if g == 0:
+                    sums[0, 0, t] = new_bank("sums")
+                mx_pass(sums[0, 0, t][:], ("adj", g, 0), t, ("dz2", g, 0), g == 0, g == G - 1)
+
+        def propagate(j, c, tiles):
+            for t in tiles:
+                sums[j, c, t] = new_bank("sums")
+                for g in range(G):
+                    mx_pass(sums[j, c, t][:], ("adj", g, j), t, ("dz2", g, c), g == 0, g == G - 1)
+
+        def mark(j, c):
+            marks[j, c] = work.tile([P, ROWS], F32, name="mark")
+            nc.vector.tensor_copy(out=marks[j, c][:], in_=r2_sb[:, j, :])
+
+        def self_term(engine, j, c, tiles):
+            for t in tiles:
+                x = work.tile([P, W], F32, name="self_loop", bufs=8)
+                src = raw["go", j, c][:, t, :]
+                if engine == GP:
+                    nc.gpsimd.tensor_scalar(out=x[:], in0=src, scalar1=marks[j, c][:, t : t + 1], scalar2=0.0,
+                                            op0=MULT, op1=ADD)
+                elif engine == V:
+                    nc.vector.tensor_scalar(out=x[:], in0=src, scalar1=r2_sb[:, j, t : t + 1], scalar2=None, op0=MULT)
+                else:
+                    nc.scalar.activation(out=x[:], in_=src, func=COPY, scale=r2_sb[:, j, t : t + 1])
+                self_loop[j, c, t] = x
+
+        def make_dz1(j, c, tiles):
+            for t in tiles:
+                if (j, c) not in dz1:
+                    dz1[j, c] = work.tile([P, ROWS, W], BF16, name="dz1", bufs=3, align_bytes=64)
+                nc.vector.scalar_tensor_tensor(out=dz1[j, c][:, t, :], in0=sums[j, c, t][:],
+                                               scalar=r_sb[:, j, t : t + 1], in1=self_loop[j, c, t][:],
+                                               op0=MULT, op1=ADD)
+
+        def turn(j, c, tag):
+            for half in range(2):
+                bank = new_bank(tag)[:].rearrange("p (k u m) -> p k u m", k=2, u=2)
+                for k in range(2):
+                    words = dz1[j, c][:, 2 * half + k, :].bitcast(F32)
+                    for u in range(2):
+                        nc.tensor.transpose(bank[:, k, u, :], words[:, u::2], ident[:])
+                flipped[j, c, half] = bank
+
+        def turned(engine, j, c):
+            grouped["feats", j, c] = work.tile([P, W, ROWS], BF16, name="grouped_feats", align_bytes=64)
+            dst = grouped["feats", j, c][:].rearrange("p w i -> p (w i)").bitcast(F32)
+            dst = dst.rearrange("p (h k m u) -> p h k m u", h=2, k=2, u=2)
+            for half in range(2):
+                copy_on[engine](out=dst[:, half], in_=flipped[j, c, half].rearrange("p k u m -> p k m u"))
+
+        def grad_h1(j, tag):
+            for t in ALL:
+                sums["h1", j, t] = new_bank(tag)
+                for c in range(C):
+                    mx_pass(sums["h1", j, t][:], ("feats", j, c), t, ("W2", c), c == 0, c == C - 1)
+
+        def store_h1_grad(j):
+            rows0[j] = work.tile([P, ROWS, W], F32, name="rows0")
+            step = 1 if j == LAST_STORED else 2
+            for t in ALL:
+                nc.scalar.copy(out=rows0[j][:, t, :], in_=sums["h1", j, t][:])
+                if (t + 1) % step == 0:
+                    part = slice(t + 1 - step, t + 1)
+                    nc.sync.dma_start(out=out0_v[j][:, part, :], in_=rows0[j][:, part, :])
+
+        def grad_w2(block, passes, tag):
+            for g in passes:
+                if g == 0:
+                    sums["W2", block] = new_bank(tag)
+                mx_pass(sums["W2", block][:], ("nodes", g, block // 4), block % 4, ("h1", g), g == 0, g == G - 1)
+
+        def store_w2_grad(engine, block):
+            x = work.tile([P, W], F32, name="rows1", bufs=4)
+            copy_on[engine](out=x[:], in_=sums["W2", block][:])
+            nc.sync.dma_start(out=out_1[P * block : P * block + P, :], in_=x[:])
+
+        nc.scalar.dma_start(out=r_sb[:], in_=r.rearrange("(g p i) -> p g i", p=P, i=ROWS))
         for g in range(G):
-            load_go(g, 0)
+            load_grad_out(g, 0)
             load_adj(g, 0)
+        for j in (1, 2):
+            for g in range(G):
+                load_adj(g, j)
         for g in range(G):
-            load_adj(g, 1)
-        for g in range(G):
-            load_adj(g, 2)
-        for g in range(G):
-            load_go(g, 1)
-
+            load_grad_out(g, 1)
+        make_identity(nc, ident_b[:])
         make_identity(nc, ident[:])
         nc.vector.tensor_tensor(out=r2_sb[:], in0=r_sb[:], in1=r_sb[:], op=MULT)
 
-        def copy_on(eng, out, in_):
-            if eng == "v":
-                nc.vector.tensor_copy(out=out, in_=in_)
-            else:
-                nc.scalar.copy(out=out, in_=in_)
+        scale_by_r(0, 0)
+        self_term(V, 0, 0, (0, 1))
+        interleave(VS, ("dz2", 0, 0))
+        interleave(S, ("adj", 0, 0))
+        load(("h1", 0), h1_v[0])
+        quantise(("dz2", 0, 0))
+        scale_by_r(1, 0)
+        mark(1, 0)
+        self_term(S, 0, 0, (2, 3))
+        interleave(V, ("dz2", 1, 0))
+        quantise(("adj", 0, 0))
+        scale_by_r(2, 0)
+        move(("adj", 1, 0))
+        load(("h1", 1), h1_v[1])
+        move(("adj", 2, 0))
+        load(("h1", 2), h1_v[2])
+        quantise(("dz2", 1, 0))
+        moved(("adj", 1, 0), (0, 1))
+        mark(2, 0)
+        interleave(VS, ("dz2", 2, 0))
+        moved(("adj", 2, 0), (0, 1))
+        quantise(("adj", 1, 0))
+        quantise(("dz2", 2, 0))
+        interleave(V, ("adj", 0, 1))
+        load(("W2", 0), w2_v[0])
+        quantise(("adj", 2, 0))
+        first_pass(0)
+        interleave(VS, ("adj", 1, 1))
+        load(("W2", 1), w2_v[1])
+        self_term(GP, 1, 0, (3,))
+        first_pass(1)
+        first_pass(2)
+        interleave(S, ("adj", 2, 1))
+        quantise(("adj", 0, 1))
 
-        def scale(g, c):
-            t = work.tile([P, 4, 512], BF16, name="dz2b", align_bytes=64)
-            for i in range(4):
-                nc.vector.tensor_scalar(out=t[:, i, :], in0=go_sb[g, c][:, i, :],
-                                        scalar1=r_sb[:, g, i : i + 1], scalar2=None, op0=MULT)
-            dz2b[g, c] = t
+        make_dz1(0, 0, ALL)
+        self_term(GP, 1, 0, (0, 1, 2))
+        move(("adj", 0, 2))
+        moved(("adj", 0, 2), (0,))
+        quantise(("adj", 1, 1))
+        quantise(("adj", 2, 1))
+        interleave(VS, ("adj", 1, 2))
+        interleave(VS, ("adj", 2, 2))
+        quantise(("adj", 1, 2))
+        interleave(VS, ("nodes", 0, 0))
+        scale_by_r(0, 1)
+        scale_by_r(1, 1)
+        scale_by_r(2, 1)
+        quantise(("adj", 2, 2))
+        moved(("adj", 0, 2), (1,))
+        self_term(GP, 2, 0, ALL)
+        mark(0, 1)
+        quantise(("adj", 0, 2))
+        turn(0, 0, "mixed")
+        mark(2, 1)
+        propagate(1, 0, ALL)
+        turned(S, 0, 0)
+        interleave(S, ("dz2", 1, 1))
+        interleave(S, ("dz2", 2, 1))
 
-        def interleave(eng, key, src):
-            t = work.tile([P, 512, 4], BF16, name="grouped", bufs=5, align_bytes=64)
-            copy_on(eng, t[:].rearrange("p (c i) t -> p c t i", i=4), src.rearrange("p t (c i) -> p c t i", i=4))
-            grouped[key] = t
+        make_dz1(1, 0, (3, 0, 1, 2))
+        move(("dz2", 0, 1))
+        quantise(("dz2", 1, 1))
+        moved(("dz2", 0, 1), (0, 1))
+        propagate(2, 0, ALL)
+        make_dz1(2, 0, (0, 1, 2))
+        quantise(("dz2", 2, 1))
+        quantise(("dz2", 0, 1))
+        turn(1, 0, "sums")
+        make_dz1(2, 0, (3,))
+        quantise(("nodes", 0, 0))
+        interleave(VS, ("h1", 1))
+        turned(S, 1, 0)
+        self_term(GP, 0, 1, ALL)
+        quantise(("feats", 1, 0))
+        propagate(0, 1, ALL)
+        mark(1, 1)
 
-        def interleave_adj(eng, key):
-            t = work.tile([P, 512, 4], BF16, name="grouped", bufs=5, align_bytes=64)
-            copy_on(eng, t[:].rearrange("p (t m) i -> p m i t", t=4), raw[key][:].rearrange("p i (m t) -> p m i t", t=4))
-            grouped[key] = t
+        make_dz1(0, 1, ALL)
+        interleave(S, ("W2", 1))
+        quantise(("W2", 1))
+        quantise(("h1", 1))
+        interleave(S, ("W2", 0))
+        propagate(2, 1, (2, 3))
+        self_term(GP, 2, 1, ALL)
+        interleave(VS, ("nodes", 1, 0))
+        turn(2, 0, "mixed")
+        quantise(("feats", 0, 0))
+        make_dz1(2, 1, (2, 3))
+        turn(0, 1, "mixed")
+        turned(V, 0, 1)
+        propagate(2, 1, (0, 1))
+        propagate(1, 1, (0, 1))
+        make_dz1(2, 1, (0, 1))
+        interleave(S, ("nodes", 2, 0))
+        quantise(("feats", 0, 1))
+        turned(S, 2, 0)
+        turn(2, 1, "sums")
+        quantise(("W2", 0))
+        interleave(VS, ("h1", 2))
+        self_term(GP, 1, 1, ALL)
+        quantise(("nodes", 1, 0))
+        quantise(("h1", 2))
+        grad_h1(0, "mixed")
+        make_dz1(1, 1, (0, 1))
+        quantise(("nodes", 2, 0))
+        propagate(1, 1, (2, 3))
+        interleave(S, ("h1", 0))
+        quantise(("h1", 0))
+        turned(S, 2, 1)
+        store_h1_grad(0)
+        quantise(("feats", 2, 1))
 
-        def quant(key, fmt):
-            tag = "_".join([str(k) for k in key])
-            c = keep.tile([P, 512], U32, name="codes_" + tag, align_bytes=64)
-            s = keep.tile([P, 512], U8, name="scales_" + tag, align_bytes=64)
-            nc.vector.quantize_mx(out=c[:].bitcast(fmt), scales=s[:], in_=grouped[key][:].rearrange("p w t -> p (w t)"))
-            codes[key] = (c, s, fmt)
-
-        def prep(eng, key):
-            if key[0] == "a":
-                interleave_adj(eng, key)
-            elif key[0] == "z":
-                interleave(eng, key, dz2b[key[1:]][:])
-            else:
-                interleave(eng, key, raw[key][:])
-
-        def mx(out, left, m0, right, start, stop):
-            lc, ls, lf = codes[left]
-            rc, rs, rf = codes[right]
-            nc.tensor.matmul_mx(out=out, lhsT=lc[:, m0 : m0 + P].bitcast(lf), lhsT_scale=ls[:, m0 : m0 + P],
-                                rhs=rc[:].bitcast(rf), rhs_scale=rs[:], start=start, stop=stop)
-
-        def new_misc():
-            return psum.tile([P, 512], F32, name="misc", bufs=4)
-
-        def new_acc():
-            return psum.tile([P, 512], F32, name="acc", bufs=4)
-
-        def r_open(j, c):
-            for t in range(4):
-                acc[j, c, t] = new_acc()
-
-        def r_pass(j, c, t, g):
-            mx(acc[j, c, t][:], ("a", g, j), P * t, ("z", g, c), g == 0, g == G - 1)
-
-        def r_group(j, c, t):
-            acc[j, c, t] = new_acc()
-            for g in range(G):
-                r_pass(j, c, t, g)
-
-        def make_q(j, c, t, eng="v"):
-            x = work.tile([P, 512], F32, name="q", bufs=6)
-            dst = x[:]
-            src = go_sb[j, c][:, t, :]
-            if eng == "v":
-                nc.vector.tensor_scalar(out=dst, in0=src, scalar1=r2_sb[:, j, t : t + 1], scalar2=None, op0=MULT)
-            else:
-                nc.scalar.activation(out=dst, in_=src, func=COPY, scale=r2_sb[:, j, t : t + 1])
-            q[j, c, t] = x
-
-        def stt(j, c, t):
-            if (j, c) not in dz1:
-                dz1[j, c] = work.tile([P, 4, 512], BF16, name="dz1", bufs=3, align_bytes=64)
-            nc.vector.scalar_tensor_tensor(out=dz1[j, c][:, t, :], in0=acc[j, c, t][:], scalar=r_sb[:, j, t : t + 1],
-                                           in1=q[j, c, t][:], op0=MULT, op1=ADD)
-
-        xt = {}
-
-        def turn(j, c, half):
-            x = new_misc()[:].rearrange("p (k u m) -> p k u m", k=2, u=2)
-            for k in range(2):
-                words = dz1[j, c][:, 2 * half + k, :].bitcast(F32)
-                for u in range(2):
-                    nc.tensor.transpose(x[:, k, u, :], words[:, u::2], ident[:])
-            xt[j, c, half] = x
-
-        def turn_out(eng, j, c, half):
-            key = ("c", j, c)
-            if key not in grouped:
-                grouped[key] = work.tile([P, 512, 4], BF16, name="grouped_c", bufs=2, align_bytes=64)
-            dst = grouped[key][:].rearrange("p w t -> p (w t)").bitcast(F32)
-            copy_on(eng, dst.rearrange("p (h k m u) -> p h k m u", h=2, k=2, u=2)[:, half],
-                    xt[j, c, half].rearrange("p k u m -> p k m u"))
-
-        o0 = {}
-
-        def out0_group(j, t):
-            a = new_misc()
-            for c in range(CH):
-                mx(a[:], ("c", j, c), P * t, ("w", c), c == 0, c == CH - 1)
-            acc["o0", j, t] = a
-
-        def out0_evac(eng, j, t):
-            if j not in o0:
-                o0[j] = work.tile([P, 4, 512], F32, name="o0", bufs=2)
-            copy_on(eng, o0[j][:, t, :], acc["o0", j, t][:])
-            if t % 2 == 1:
-                nc.sync.dma_start(out=out0_v[j][:, t - 1 : t + 1, :], in_=o0[j][:, t - 1 : t + 1, :])
-
-        def out1_pass(cb, g, new):
-            if g == 0:
-                acc["o1", cb] = new()
-            mx(acc["o1", cb][:], ("n", g, cb // 4), P * (cb % 4), ("h", g), g == 0, g == G - 1)
-
-        def out1_evac(eng, cb):
-            x = work.tile([P, 512], F32, name="o1", bufs=4)
-            copy_on(eng, x[:], acc["o1", cb][:])
-            nc.sync.dma_start(out=out_1[P * cb : P * cb + P, :], in_=x[:])
-
-        rounds = [(j, c) for c in range(CH) for j in range(G)]
-
-        def r_passes(k, g):
-            for t in range(4):
-                r_pass(*rounds[k], t, g)
-
-        r_open(0, 0)
-        for g in range(G):
-            scale(g, 0)
-            if g:
-                quant(("z", g - 1, 0), E5M2)
-            prep("v", ("z", g, 0))
-            prep("s", ("a", g, 0))
-            if g:
-                quant(("a", g - 1, 0), E4M3)
-                r_passes(0, g - 1)
-        for t in range(4):
-            make_q(0, 0, t, "s")
-        prep("v", ("a", 0, 1))
-        quant(("z", 2, 0), E5M2)
-        quant(("a", 2, 0), E4M3)
-        r_passes(0, 2)
-        quant(("a", 0, 1), E4M3)
-
-        extra = [
-            [("a", 1, 1, "s"), ("a", 2, 1, "s")],
-            [("a", 0, 2, "s"), ("a", 1, 2, "s"), ("a", 2, 2, "v")],
-            [("z", 0, 1, "s"), ("z", 1, 1, "v"), ("z", 2, 1, "s")],
-            [("h", 0, "v"), ("h", 1, "s"), ("h", 2, "s")],
-            [("w", 0, "v"), ("w", 1, "s")],
-            [],
-        ]
-        for k in range(6):
-            j, c = rounds[k]
-            if k == 1:
-                for g in range(G):
-                    load(("h", g), h1_v[g])
-                for g in range(CH):
-                    load(("w", g), w2_v[g])
-            for e in extra[k]:
-                if e[0] == "z":
-                    scale(*e[1:3])
-                if e[-1] == "s":
-                    prep(e[-1], e[:-1])
-            for t in range(4):
-                stt(j, c, t)
-            for e in extra[k]:
-                if e[-1] == "v":
-                    prep(e[-1], e[:-1])
-            if k > 0:
-                quant(("c", *rounds[k - 1]), E5M2)
-            if k < 5:
-                for t in range(4):
-                    make_q(*rounds[k + 1], t, "s")
-            if k == 0:
-                interleave("v", ("n", j, c), dz1[j, c][:])
-            for e in extra[k]:
-                quant(e[:-1], E5M2 if e[0] == "z" else E4M3)
-            if k > 0:
-                interleave("v", ("n", j, c), dz1[j, c][:])
-            if k < 5:
-                for t in range(4):
-                    r_group(*rounds[k + 1], t)
-            else:
-                for g in range(2):
-                    for cb in range(4, 8):
-                        out1_pass(cb, g, new_acc)
-            for half in range(2):
-                turn(j, c, half)
-            for half in range(2):
-                turn_out("s", j, c, half)
-            if k == 4:
-                for cb in range(4):
-                    for g in range(G):
-                        out1_pass(cb, g, new_misc)
-                    out1_evac("s", cb)
-                for t in range(4):
-                    out0_group(0, t)
-                    out0_evac("s", 0, t)
-            if k == 5:
-                for t in range(4):
-                    out0_group(1, t)
-                    out0_evac("s", 1, t)
-                quant(("c", *rounds[5]), E5M2)
-            quant(("n", j, c), E5M2)
-        for t in range(4):
-            out0_group(2, t)
-            out0_evac("sv"[t % 2], 2, t)
-        for cb in range(4, 8):
-            out1_pass(cb, 2, new_acc)
-            out1_evac("sv"[cb % 2], cb)
+        grad_w2(1, (0, 1, 2), "sums")
+        grad_w2(2, (0, 1, 2), "sums")
+        quantise(("feats", 2, 0))
+        make_dz1(1, 1, (2, 3))
+        turn(1, 1, "mixed")
+        turned(V, 1, 1)
+        store_w2_grad(S, 1)
+        store_w2_grad(S, 2)
+        grad_h1(2, "sums")
+        interleave(VS, ("nodes", 2, 1))
+        quantise(("feats", 1, 1))
+        interleave(V, ("nodes", 1, 1))
+        store_h1_grad(2)
+        interleave(VS, ("nodes", 0, 1))
+        grad_w2(0, (0, 1, 2), "sums")
+        grad_w2(3, (0, 1, 2), "mixed")
+        store_w2_grad(V, 0)
+        quantise(("nodes", 0, 1))
+        quantise(("nodes", 1, 1))
+        grad_h1(1, "sums")
+        quantise(("nodes", 2, 1))
+        grad_w2(5, (0, 1), "mixed")
+        grad_w2(6, (0, 1, 2), "mixed")
+        grad_w2(7, (0, 1, 2), "mixed")
+        grad_w2(5, (2,), "mixed")
+        store_w2_grad(S, 3)
+        store_h1_grad(1)
+        store_w2_grad(V, 6)
+        store_w2_grad(V, 7)
+        grad_w2(4, (0, 1, 2), "mixed")
+        store_w2_grad(V, 5)
+        store_w2_grad(S, 4)

from contextlib import ExitStack

import concourse.mybir as mybir
from concourse.masks import make_identity

NODES, HID, OUT_F = 1536, 512, 1024
FLOPS = 2 * NODES * NODES * OUT_F + 2 * (2 * NODES * OUT_F * HID)
BYTES = 2 * (NODES * NODES + NODES * OUT_F + OUT_F * HID + NODES * HID) + 4 * (NODES + NODES * HID + OUT_F * HID)

F32 = mybir.dt.float32
BF16 = mybir.dt.bfloat16
U32 = mybir.dt.uint32
U8 = mybir.dt.uint8
E4M3 = mybir.dt.float8_e4m3fn_x4
E5M2 = mybir.dt.float8_e5m2_x4
MULT = mybir.AluOpType.mult
ADD = mybir.AluOpType.add
COPY = mybir.ActivationFunctionType.Copy

P = 128
ROWS = 4
W = P * ROWS
TILES = W // P
G = NODES // W
C = OUT_F // W
BANKS = 4

V, S, GP, VS = "v", "s", "g", "vs"
ALL = (0, 1, 2, 3)
LAST_STORED = 1


def tile_gcnlayer_pa_v_kernel(tc, h1, adj, W2, b2, r, grad_out, out_0, out_1):
    nc = tc.nc
    copy_on = {V: nc.vector.tensor_copy, S: nc.scalar.copy}

    adj_v = adj.rearrange("(g p i) j -> g p i j", p=P, i=ROWS)
    go_v = grad_out.rearrange("(g p i) c -> g p i c", p=P, i=ROWS)
    h1_v = h1.rearrange("(g p i) h -> g p i h", p=P, i=ROWS)
    w2_v = W2.rearrange("(g p i) h -> g p i h", p=P, i=ROWS)
    out0_v = out_0.rearrange("(g p i) h -> g p i h", p=P, i=ROWS)

    with ExitStack() as ctx:
        keep = ctx.enter_context(tc.tile_pool(name="keep", bufs=1))
        rawp = ctx.enter_context(tc.tile_pool(name="raw", bufs=9))
        work = ctx.enter_context(tc.tile_pool(name="work", bufs=2))
        psum = ctx.enter_context(tc.psum_pool(name="psum", bufs=BANKS))
        ctx.enter_context(tc.manual_schedule())

        r_sb = keep.tile([P, G, ROWS], F32, name="r_sb")
        r2_sb = keep.tile([P, G, ROWS], F32, name="r2_sb")
        ident = keep.tile([P, P], F32, name="ident")
        ident_b = keep.tile([P, P], BF16, name="ident_b")

        raw = {}
        grouped = {}
        codes = {}
        moving = {}
        dz1 = {}
        self_loop = {}
        marks = {}
        sums = {}
        flipped = {}
        rows0 = {}

        def load(key, view):
            raw[key] = rawp.tile([P, ROWS, W], BF16, name="raw_chunk", align_bytes=64)
            nc.sync.dma_start(out=raw[key][:], in_=view)

        def load_adj(g, j):
            load(("adj", g, j), adj_v[g][:, :, W * j : W * j + W])

        def load_grad_out(g, c):
            raw["go", g, c] = keep.tile([P, ROWS, W], BF16, name="go_%d_%d" % (g, c), align_bytes=64)
            nc.sync.dma_start(out=raw["go", g, c][:], in_=go_v[g][:, :, W * c : W * c + W])

        def scale_by_r(g, c):
            raw["dz2", g, c] = work.tile([P, ROWS, W], BF16, name="dz2", bufs=3, align_bytes=64)
            for i in range(ROWS):
                nc.vector.tensor_scalar(out=raw["dz2", g, c][:, i, :], in0=raw["go", g, c][:, i, :],
                                        scalar1=r_sb[:, g, i : i + 1], scalar2=None, op0=MULT)

        def new_grouped():
            return work.tile([P, W, ROWS], BF16, name="grouped", bufs=6, align_bytes=64)

        def interleave(engines, key):
            grouped[key] = new_grouped()
            if key[0] == "adj":
                dst = grouped[key][:].rearrange("p (t a m) i -> p a t m i", t=TILES, m=2)
                src = raw[key][:].rearrange("p i (a m t) -> p a t m i", m=2, t=TILES)
                share = TILES // len(engines)
                for n, e in enumerate(engines):
                    part = slice(share * n, share * n + share)
                    copy_on[e](out=dst[:, :, part], in_=src[:, :, part])
            else:
                dst = grouped[key][:].rearrange("p (w n) i -> p w i n", n=4)
                src = (dz1[key[1:]] if key[0] == "nodes" else raw[key])[:].rearrange("p i (w n) -> p w i n", n=4)
                share = W // 4 // len(engines)
                for n, e in enumerate(engines):
                    part = slice(share * n, share * n + share)
                    copy_on[e](out=dst[:, part], in_=src[:, part])

        def move(key):
            for half in range(2):
                bank = psum.tile([P, ROWS * W // 2], BF16, name="mixed")
                cols = slice(W // 2 * half, W // 2 * half + W // 2)
                if key[0] == "adj":
                    dst = bank[:].rearrange("p (t m i) -> p i m t", t=TILES, i=ROWS)
                else:
                    dst = bank[:].rearrange("p (w i) -> p i w", i=ROWS)
                for i in range(0, ROWS, 2):
                    src = raw[key][:, i : i + 2, cols]
                    if key[0] == "adj":
                        src = src.rearrange("p i (m t) -> p i m t", t=TILES)
                    nc.tensor.matmul(dst[:, i : i + 2], lhsT=ident_b[:], rhs=src, start=True, stop=True)
                moving[key, half] = bank

        def moved(key, halves):
            for half in halves:
                if half == 0:
                    grouped[key] = new_grouped()
                cols = slice(W // 2 * half, W // 2 * half + W // 2)
                bank = moving[key, half]
                if key[0] == "adj":
                    dst = grouped[key][:].rearrange("p (t m) i -> p t (m i)", t=TILES)[:, :, cols]
                    nc.scalar.copy(out=dst, in_=bank[:].rearrange("p (t n) -> p t n", t=TILES))
                else:
                    nc.scalar.copy(out=grouped[key][:, cols, :].rearrange("p w i -> p (w i)"), in_=bank[:])

        def quantise(key):
            fmt = E5M2 if key[0] in ("dz2", "nodes", "feats") else E4M3
            tag = "_".join([str(k) for k in key])
            words = keep.tile([P, W], U32, name="words_" + tag, align_bytes=64)
            scales = keep.tile([P, W], U8, name="scales_" + tag, align_bytes=64)
            nc.vector.quantize_mx(out=words[:].bitcast(fmt), scales=scales[:],
                                  in_=grouped[key][:].rearrange("p w i -> p (w i)"))
            codes[key] = (words, scales, fmt)

        def mx_pass(out, left, block, right, start, stop):
            lw, ls, lf = codes[left]
            rw, rs, rf = codes[right]
            cols = slice(P * block, P * block + P)
            nc.tensor.matmul_mx(out=out, lhsT=lw[:, cols].bitcast(lf), lhsT_scale=ls[:, cols],
                                rhs=rw[:].bitcast(rf), rhs_scale=rs[:], start=start, stop=stop)

        def new_bank(tag):
            return psum.tile([P, W], F32, name=tag)

        def first_pass(g):
            for t in ALL:
                if g == 0:
                    sums[0, 0, t] = new_bank("sums")
                mx_pass(sums[0, 0, t][:], ("adj", g, 0), t, ("dz2", g, 0), g == 0, g == G - 1)

        def propagate(j, c, tiles):
            for t in tiles:
                sums[j, c, t] = new_bank("sums")
                for g in range(G):
                    mx_pass(sums[j, c, t][:], ("adj", g, j), t, ("dz2", g, c), g == 0, g == G - 1)

        def mark(j, c):
            marks[j, c] = work.tile([P, ROWS], F32, name="mark")
            nc.vector.tensor_copy(out=marks[j, c][:], in_=r2_sb[:, j, :])

        def self_term(engine, j, c, tiles):
            for t in tiles:
                x = work.tile([P, W], F32, name="self_loop", bufs=8)
                src = raw["go", j, c][:, t, :]
                if engine == GP:
                    nc.gpsimd.tensor_scalar(out=x[:], in0=src, scalar1=marks[j, c][:, t : t + 1], scalar2=0.0,
                                            op0=MULT, op1=ADD)
                elif engine == V:
                    nc.vector.tensor_scalar(out=x[:], in0=src, scalar1=r2_sb[:, j, t : t + 1], scalar2=None, op0=MULT)
                else:
                    nc.scalar.activation(out=x[:], in_=src, func=COPY, scale=r2_sb[:, j, t : t + 1])
                self_loop[j, c, t] = x

        def make_dz1(j, c, tiles):
            for t in tiles:
                if (j, c) not in dz1:
                    dz1[j, c] = work.tile([P, ROWS, W], BF16, name="dz1", bufs=3, align_bytes=64)
                nc.vector.scalar_tensor_tensor(out=dz1[j, c][:, t, :], in0=sums[j, c, t][:],
                                               scalar=r_sb[:, j, t : t + 1], in1=self_loop[j, c, t][:],
                                               op0=MULT, op1=ADD)

        def turn(j, c, tag):
            for half in range(2):
                bank = new_bank(tag)[:].rearrange("p (k u m) -> p k u m", k=2, u=2)
                for k in range(2):
                    words = dz1[j, c][:, 2 * half + k, :].bitcast(F32)
                    for u in range(2):
                        nc.tensor.transpose(bank[:, k, u, :], words[:, u::2], ident[:])
                flipped[j, c, half] = bank

        def turned(engine, j, c):
            grouped["feats", j, c] = work.tile([P, W, ROWS], BF16, name="grouped_feats", align_bytes=64)
            dst = grouped["feats", j, c][:].rearrange("p w i -> p (w i)").bitcast(F32)
            dst = dst.rearrange("p (h k m u) -> p h k m u", h=2, k=2, u=2)
            for half in range(2):
                copy_on[engine](out=dst[:, half], in_=flipped[j, c, half].rearrange("p k u m -> p k m u"))

        def grad_h1(j, tag):
            for t in ALL:
                sums["h1", j, t] = new_bank(tag)
                for c in range(C):
                    mx_pass(sums["h1", j, t][:], ("feats", j, c), t, ("W2", c), c == 0, c == C - 1)

        def store_h1_grad(j):
            rows0[j] = work.tile([P, ROWS, W], F32, name="rows0")
            step = 1 if j == LAST_STORED else 2
            for t in ALL:
                nc.scalar.copy(out=rows0[j][:, t, :], in_=sums["h1", j, t][:])
                if (t + 1) % step == 0:
                    part = slice(t + 1 - step, t + 1)
                    nc.sync.dma_start(out=out0_v[j][:, part, :], in_=rows0[j][:, part, :])

        def grad_w2(block, passes, tag):
            for g in passes:
                if g == 0:
                    sums["W2", block] = new_bank(tag)
                mx_pass(sums["W2", block][:], ("nodes", g, block // 4), block % 4, ("h1", g), g == 0, g == G - 1)

        def store_w2_grad(engine, block):
            x = work.tile([P, W], F32, name="rows1", bufs=4)
            copy_on[engine](out=x[:], in_=sums["W2", block][:])
            nc.sync.dma_start(out=out_1[P * block : P * block + P, :], in_=x[:])

        nc.scalar.dma_start(out=r_sb[:], in_=r.rearrange("(g p i) -> p g i", p=P, i=ROWS))
        for g in range(G):
            load_grad_out(g, 0)
            load_adj(g, 0)
        for j in (1, 2):
            for g in range(G):
                load_adj(g, j)
        for g in range(G):
            load_grad_out(g, 1)
        make_identity(nc, ident_b[:])
        make_identity(nc, ident[:])
        nc.vector.tensor_tensor(out=r2_sb[:], in0=r_sb[:], in1=r_sb[:], op=MULT)

        scale_by_r(0, 0)
        self_term(V, 0, 0, (0, 1))
        interleave(VS, ("dz2", 0, 0))
        interleave(S, ("adj", 0, 0))
        load(("h1", 0), h1_v[0])
        quantise(("dz2", 0, 0))
        scale_by_r(1, 0)
        mark(1, 0)
        self_term(S, 0, 0, (2, 3))
        interleave(V, ("dz2", 1, 0))
        quantise(("adj", 0, 0))
        scale_by_r(2, 0)
        move(("adj", 1, 0))
        load(("h1", 1), h1_v[1])
        move(("adj", 2, 0))
        load(("h1", 2), h1_v[2])
        quantise(("dz2", 1, 0))
        moved(("adj", 1, 0), (0, 1))
        mark(2, 0)
        interleave(VS, ("dz2", 2, 0))
        moved(("adj", 2, 0), (0, 1))
        quantise(("adj", 1, 0))
        quantise(("dz2", 2, 0))
        interleave(V, ("adj", 0, 1))
        load(("W2", 0), w2_v[0])
        quantise(("adj", 2, 0))
        first_pass(0)
        interleave(VS, ("adj", 1, 1))
        load(("W2", 1), w2_v[1])
        self_term(GP, 1, 0, (3,))
        first_pass(1)
        first_pass(2)
        interleave(S, ("adj", 2, 1))
        quantise(("adj", 0, 1))

        make_dz1(0, 0, ALL)
        self_term(GP, 1, 0, (0, 1, 2))
        move(("adj", 0, 2))
        moved(("adj", 0, 2), (0,))
        quantise(("adj", 1, 1))
        quantise(("adj", 2, 1))
        interleave(VS, ("adj", 1, 2))
        interleave(VS, ("adj", 2, 2))
        quantise(("adj", 1, 2))
        interleave(VS, ("nodes", 0, 0))
        scale_by_r(0, 1)
        scale_by_r(1, 1)
        scale_by_r(2, 1)
        quantise(("adj", 2, 2))
        moved(("adj", 0, 2), (1,))
        self_term(GP, 2, 0, ALL)
        mark(0, 1)
        quantise(("adj", 0, 2))
        turn(0, 0, "mixed")
        mark(2, 1)
        propagate(1, 0, ALL)
        turned(S, 0, 0)
        interleave(S, ("dz2", 1, 1))
        interleave(S, ("dz2", 2, 1))

        make_dz1(1, 0, (3, 0, 1, 2))
        move(("dz2", 0, 1))
        quantise(("dz2", 1, 1))
        moved(("dz2", 0, 1), (0, 1))
        propagate(2, 0, ALL)
        make_dz1(2, 0, (0, 1, 2))
        quantise(("dz2", 2, 1))
        quantise(("dz2", 0, 1))
        turn(1, 0, "sums")
        make_dz1(2, 0, (3,))
        quantise(("nodes", 0, 0))
        interleave(VS, ("h1", 1))
        turned(S, 1, 0)
        self_term(GP, 0, 1, ALL)
        quantise(("feats", 1, 0))
        propagate(0, 1, ALL)
        mark(1, 1)

        make_dz1(0, 1, ALL)
        interleave(S, ("W2", 1))
        quantise(("W2", 1))
        quantise(("h1", 1))
        interleave(S, ("W2", 0))
        propagate(2, 1, (2, 3))
        self_term(GP, 2, 1, ALL)
        interleave(VS, ("nodes", 1, 0))
        turn(2, 0, "mixed")
        quantise(("feats", 0, 0))
        make_dz1(2, 1, (2, 3))
        turn(0, 1, "mixed")
        turned(V, 0, 1)
        propagate(2, 1, (0, 1))
        propagate(1, 1, (0, 1))
        make_dz1(2, 1, (0, 1))
        interleave(S, ("nodes", 2, 0))
        quantise(("feats", 0, 1))
        turned(S, 2, 0)
        turn(2, 1, "sums")
        quantise(("W2", 0))
        interleave(VS, ("h1", 2))
        self_term(GP, 1, 1, ALL)
        quantise(("nodes", 1, 0))
        quantise(("h1", 2))
        grad_h1(0, "mixed")
        make_dz1(1, 1, (0, 1))
        quantise(("nodes", 2, 0))
        propagate(1, 1, (2, 3))
        interleave(S, ("h1", 0))
        quantise(("h1", 0))
        turned(S, 2, 1)
        store_h1_grad(0)
        quantise(("feats", 2, 1))

        grad_w2(1, (0, 1, 2), "sums")
        grad_w2(2, (0, 1, 2), "sums")
        quantise(("feats", 2, 0))
        make_dz1(1, 1, (2, 3))
        turn(1, 1, "mixed")
        turned(V, 1, 1)
        store_w2_grad(S, 1)
        store_w2_grad(S, 2)
        grad_h1(2, "sums")
        interleave(VS, ("nodes", 2, 1))
        quantise(("feats", 1, 1))
        interleave(V, ("nodes", 1, 1))
        store_h1_grad(2)
        interleave(VS, ("nodes", 0, 1))
        grad_w2(0, (0, 1, 2), "sums")
        grad_w2(3, (0, 1, 2), "mixed")
        store_w2_grad(V, 0)
        quantise(("nodes", 0, 1))
        quantise(("nodes", 1, 1))
        grad_h1(1, "sums")
        quantise(("nodes", 2, 1))
        grad_w2(5, (0, 1), "mixed")
        grad_w2(6, (0, 1, 2), "mixed")
        grad_w2(7, (0, 1, 2), "mixed")
        grad_w2(5, (2,), "mixed")
        store_w2_grad(S, 3)
        store_h1_grad(1)
        store_w2_grad(V, 6)
        store_w2_grad(V, 7)
        grad_w2(4, (0, 1, 2), "mixed")
        store_w2_grad(V, 5)
        store_w2_grad(S, 4)
